import numpy as np
import ml_dtypes


def mxq(x, axis, fmt="e4m3"):
    dtype, down = {"e4m3": (ml_dtypes.float8_e4m3fn, 7), "e5m2": (ml_dtypes.float8_e5m2, 14)}[fmt]
    v = np.moveaxis(np.asarray(x, np.float32).astype(ml_dtypes.bfloat16).astype(np.float64), axis, -1)
    blocks = v.reshape(v.shape[:-1] + (-1, 32))
    amax = np.abs(blocks).max(-1, keepdims=True)
    byte = np.maximum(np.where(amax > 0, np.frexp(amax)[1] - 1 + 127, 0) - down, 1)
    scale = np.exp2(byte - 127.0)
    codes = (blocks / scale).astype(np.float32).astype(dtype).astype(np.float64)
    return np.moveaxis((codes * scale).reshape(v.shape), -1, axis)


WIDE = False


def mx_kscale(k):
    if not WIDE:
        return np.ones(k)
    levels = np.array([10, -10, 5, -5, 0])
    a = np.random.permutation(np.resize(levels, k // 512 * 4)).reshape(k // 512, 4)
    idx = np.arange(k)
    return np.exp2(a[idx // 512, idx % 128 // 32])


BF16 = ml_dtypes.bfloat16


def bf(x):
    return np.asarray(x, np.float32).astype(BF16)


def f64(x):
    return np.asarray(x).astype(np.float64)


E2M1 = np.array([0.0, 0.5, 1.0, 1.5, 2.0, 3.0, 4.0, 6.0, -0.0, -0.5, -1.0, -1.5, -2.0, -3.0, -4.0, -6.0])


def pack_weight(w, fmt):
    k, n = w.shape
    w = f64(bf(w)).reshape(k // 32, 32, n)
    amax = np.abs(w).max(1)
    if fmt == "e4m3":
        byte = np.frexp(amax)[1] - 1 + 127 - 7
    else:
        mant, ex = np.frexp(amax / 6.0)
        byte = np.where(mant > 0.5, ex, ex - 1) + 127
    byte = np.clip(np.where(amax > 0, byte, 1), 1, 254)
    scaled = (w * np.exp2(127.0 - byte)[:, None, :]).reshape(k, n).astype(np.float32)
    by_word = np.ascontiguousarray(scaled.reshape(k // 512, 128, 4, n).transpose(0, 1, 3, 2))
    if fmt == "e4m3":
        words = by_word.astype(ml_dtypes.float8_e4m3fn).view(np.uint8)
    else:
        c = by_word.astype(ml_dtypes.float4_e2m1fn).view(np.uint8) & 0xF
        words = c[..., 0::2] | (c[..., 1::2] << 4)
    return np.ascontiguousarray(words), np.ascontiguousarray(byte.astype(np.uint8).reshape(k // 512, 16, n))


def unpack_weight(words, scales, fmt):
    g, p, n, _ = words.shape
    if fmt == "e4m3":
        vals = np.ascontiguousarray(words).view(ml_dtypes.float8_e4m3fn).astype(np.float64)
    else:
        nib = np.empty((g, p, n, 4), np.uint8)
        nib[..., 0::2] = words & 0xF
        nib[..., 1::2] = words >> 4
        vals = E2M1[nib]
    vals = vals * np.repeat(np.exp2(scales.astype(np.float64) - 127.0), 8, axis=1)[..., None]
    return vals.transpose(0, 1, 3, 2).reshape(g * 512, n)


M, D, DI, N, KC = 128, 16384, 512, 16, 4
FMT = "e4m3"


def sigmoid(v):
    e = np.exp(-np.abs(v))
    return np.where(v >= 0, 1.0 / (1.0 + e), e / (1.0 + e))


def setup_inputs():
    s = mx_kscale(D)
    x = bf(np.random.standard_normal((M, D)) * s)
    in_w_words, in_w_scales = pack_weight(np.random.standard_normal((D, DI)) / np.sqrt(D) / s[:, None], FMT)
    in_b = bf(np.random.standard_normal(DI) * 0.1)
    conv_w = bf(np.random.standard_normal((DI, KC)) * 0.5)
    conv_b = bf(np.random.standard_normal(DI) * 0.1)
    A_log = bf(np.log(np.broadcast_to(np.arange(1, N + 1, dtype=np.float64), (DI, N))))
    B = bf(np.random.standard_normal((DI, N)) * N ** -0.25)
    C = bf(np.random.standard_normal((DI, N)) * N ** -0.25)
    Dp = bf(1.0 + 0.1 * np.random.standard_normal(DI))
    dt = bf(1.0 + 0.1 * np.random.standard_normal(DI))
    out_w_words, out_w_scales = pack_weight(np.random.standard_normal((DI, D)) / np.sqrt(DI), FMT)
    out_b = bf(np.random.standard_normal(D) * 0.1)
    return {"x": x,
            "in_w_words": in_w_words,
            "in_w_scales": in_w_scales,
            "in_b": in_b,
            "conv_w": conv_w,
            "conv_b": conv_b,
            "A_log": A_log,
            "B": B,
            "C": C,
            "Dp": Dp,
            "dt": dt,
            "out_w_words": out_w_words,
            "out_w_scales": out_w_scales,
            "out_b": out_b}


def reference(x, in_w_words, in_w_scales, in_b, conv_w, conv_b, A_log, B, C, Dp, dt, out_w_words, out_w_scales, out_b):
    xi = (mxq(f64(x), 1, "e4m3") @ unpack_weight(in_w_words, in_w_scales, FMT)) + f64(in_b)
    x_conv = xi * f64(conv_w)[:, -1] + f64(conv_b)
    delta = np.logaddexp(f64(dt), 0.0)
    A = -np.exp(f64(A_log))
    del A
    bc = np.sum(f64(B) * f64(C), axis=-1)
    y = xi * (delta * bc + f64(Dp))
    v = x_conv + y
    out = v * sigmoid(v)
    return (mxq(out, 1, "e4m3") @ unpack_weight(out_w_words, out_w_scales, FMT)) + f64(out_b)

@@ -1,0 +1,274 @@
+import concourse.mybir as mybir
+from concourse.masks import make_identity
+
+F32 = mybir.dt.float32
+BF16 = mybir.dt.bfloat16
+I32 = mybir.dt.int32
+U32 = mybir.dt.uint32
+U8 = mybir.dt.uint8
+FP8X4 = mybir.dt.float8_e4m3fn_x4
+ACT = mybir.ActivationFunctionType
+ALU = mybir.AluOpType
+AX = mybir.AxisListType
+
+P = 128
+PACK = 4
+K_PASS = P * PACK
+D = 16384
+DI = 512
+N_STATE = 16
+GROUPS = D // K_PASS
+BANK = 512
+
+X_CHUNKS = 4
+X_COLS = D // X_CHUNKS
+X_GROUPS = GROUPS // X_CHUNKS
+W_CHUNKS = 8
+W_GROUPS = GROUPS // W_CHUNKS
+O_CHUNKS = 8
+O_COLS = D // O_CHUNKS
+O_BANKS = O_COLS // BANK
+PLANES = 4
+QUADS = 4
+OW_PLANE_COLS = D // PLANES
+BIG_PER_ROUND = 2
+SMALL_PER_ROUND = 6
+BIAS_AHEAD = 2
+
+FLOPS = 2 * P * D * DI * 2
+
+
+def tile_baselinedensemamba_k_kernel(
+    tc, x, in_w_words, in_w_scales, in_b, conv_w, conv_b, A_log, B, C, Dp, dt,
+    out_w_words, out_w_scales, out_b, out,
+):
+    nc = tc.nc
+    with tc.manual_schedule(), \
+            tc.tile_pool(name="big", bufs=X_CHUNKS + W_CHUNKS + O_CHUNKS) as big, \
+            tc.tile_pool(name="keep", bufs=1) as keep, \
+            tc.tile_pool(name="stage", bufs=4) as stage, \
+            tc.tile_pool(name="biasp", bufs=BIAS_AHEAD + 1) as biasp, \
+            tc.psum_pool(name="tp", bufs=3) as tp, \
+            tc.psum_pool(name="accp", bufs=5) as accp:
+
+        in_planes = keep.tile([P, W_CHUNKS, DI], U8, align_bytes=64)
+        ow_planes = keep.tile([P, OW_PLANE_COLS], U8, align_bytes=64)
+        ob_rows = keep.tile([P, 2 * P], BF16)
+        zero_col = keep.tile([P, 1], F32)
+        nc.vector.memset(in_planes[:].rearrange("p g n -> p (g n)").bitcast(I32), 0)
+        nc.vector.memset(ow_planes[:].bitcast(I32), 0)
+        nc.vector.memset(ob_rows[:], 0.0)
+        nc.vector.memset(zero_col[:], 0.0)
+
+        ident_f32 = keep.tile([P, P], F32)
+        make_identity(nc, ident_f32[:])
+
+        dt4 = keep.tile([P, PACK], BF16)
+        b4 = keep.tile([P, PACK * N_STATE], BF16)
+        c4 = keep.tile([P, PACK * N_STATE], BF16)
+        dp4 = keep.tile([P, PACK], BF16)
+        cw4 = keep.tile([P, PACK * 4], BF16)
+        inb4 = keep.tile([P, PACK], BF16)
+        cvb4 = keep.tile([P, PACK], BF16)
+        nc.gpsimd.dma_start(out=dt4[:], in_=dt.rearrange("(p j) -> p j", j=PACK))
+        nc.gpsimd.dma_start(out=b4[:], in_=B.rearrange("(p j) n -> p (j n)", j=PACK))
+        nc.gpsimd.dma_start(out=c4[:], in_=C.rearrange("(p j) n -> p (j n)", j=PACK))
+        nc.gpsimd.dma_start(out=dp4[:], in_=Dp.rearrange("(p j) -> p j", j=PACK))
+        nc.gpsimd.dma_start(out=cw4[:], in_=conv_w.rearrange("(p j) k -> p (j k)", j=PACK))
+        nc.gpsimd.dma_start(out=inb4[:], in_=in_b.rearrange("(p j) -> p j", j=PACK))
+        nc.gpsimd.dma_start(out=cvb4[:], in_=conv_b.rearrange("(p j) -> p j", j=PACK))
+        nc.gpsimd.dma_start(out=ob_rows[0 : P // 2, :], in_=out_b.rearrange("(m w) -> m w", w=2 * P))
+        ident_bf16 = keep.tile([P, P], BF16)
+        make_identity(nc, ident_bf16[:])
+
+        big_loads = []
+        x_sb = []
+        for c in range(X_CHUNKS):
+            x_piece = big.tile([P, X_COLS], BF16, tag="mib", name="x_piece", align_bytes=64)
+            x_sb.append(x_piece)
+            big_loads.append((x_piece[:], x[:, c * X_COLS : (c + 1) * X_COLS]))
+        w_sb = []
+        for G in range(W_CHUNKS):
+            w_piece = big.tile([P, W_GROUPS, DI], U32, tag="mib", name="w_piece", align_bytes=64)
+            w_sb.append(w_piece)
+            big_loads.append((
+                w_piece[:].bitcast(I32),
+                in_w_words[G * W_GROUPS : (G + 1) * W_GROUPS].rearrange("g p n t -> p g (n t)").bitcast(I32),
+            ))
+        ow_sb = []
+        ow_flat = out_w_words[0].rearrange("p n t -> p (n t)")
+        for c in range(O_CHUNKS):
+            ow_piece = big.tile([P, O_COLS], U32, tag="mib", name="ow_piece", align_bytes=64)
+            ow_sb.append(ow_piece)
+            big_loads.append((
+                ow_piece[:].bitcast(I32),
+                ow_flat[:, c * O_COLS * PACK : (c + 1) * O_COLS * PACK].bitcast(I32),
+            ))
+
+        small_loads = []
+        for G in range(W_CHUNKS):
+            for Q in range(QUADS):
+                small_loads.append((
+                    in_planes[32 * Q : 32 * Q + 16, G, :].bitcast(I32),
+                    in_w_scales[G * PLANES : (G + 1) * PLANES, 4 * Q : 4 * Q + 4, :].bitcast(I32),
+                ))
+        for Q in range(QUADS):
+            small_loads.append((
+                ow_planes[32 * Q : 32 * Q + 16, :].bitcast(I32),
+                out_w_scales[0, 4 * Q : 4 * Q + 4, :].rearrange("r (j c) -> j r c", j=PLANES).bitcast(I32),
+            ))
+
+        rounds = len(small_loads) // SMALL_PER_ROUND
+        for r in range(rounds):
+            for dst, src in big_loads[r * BIG_PER_ROUND : (r + 1) * BIG_PER_ROUND]:
+                nc.sync.dma_start(out=dst, in_=src)
+            for dst, src in small_loads[r * SMALL_PER_ROUND : (r + 1) * SMALL_PER_ROUND]:
+                nc.sync.dma_start(out=dst, in_=src)
+        for dst, src in big_loads[rounds * BIG_PER_ROUND :]:
+            nc.sync.dma_start(out=dst, in_=src)
+
+        x_codes = keep.tile([P, GROUPS * P], U32, align_bytes=64)
+        x_planes = keep.tile([P, GROUPS * P], U8, align_bytes=64)
+        for c in range(X_CHUNKS):
+            x_words = x_sb[c][:].bitcast(F32)
+            for pair in range(X_GROUPS // 2):
+                xt = tp.tile([P, 2, 2, P], F32, tag="tp", name="xt")
+                for i in range(2):
+                    first = (2 * pair + i) * (K_PASS // 2)
+                    for u in range(2):
+                        nc.tensor.transpose(
+                            xt[:, i, u, :],
+                            x_words[:, first + u : first + K_PASS // 2 : 2],
+                            ident_f32[:],
+                        )
+                grouped = stage.tile([P, 2 * K_PASS], BF16, name="grouped", align_bytes=64)
+                nc.scalar.copy(
+                    out=grouped[:].bitcast(F32).rearrange("p (i m u) -> p i m u", i=2, u=2),
+                    in_=xt[:].rearrange("p i u m -> p i m u"),
+                )
+                col = (c * X_GROUPS + 2 * pair) * P
+                nc.vector.quantize_mx(
+                    out=x_codes[:, col : col + 2 * P].bitcast(FP8X4),
+                    scales=x_planes[:, col : col + 2 * P],
+                    in_=grouped[:],
+                )
+
+        prod = keep.tile([P, PACK * N_STATE], F32)
+        bc = keep.tile([P, PACK], F32)
+        relu_dt = keep.tile([P, PACK], F32)
+        abs_dt = keep.tile([P, PACK], F32)
+        exp_dt = keep.tile([P, PACK], F32)
+        log_dt = keep.tile([P, PACK], F32)
+        gain = keep.tile([P, PACK], F32)
+        shift = keep.tile([P, PACK], F32)
+        warm = keep.tile([P, 1], F32)
+        nc.vector.tensor_tensor(out=prod[:], in0=b4[:], in1=c4[:], op=ALU.mult)
+        nc.vector.tensor_reduce(
+            out=bc[:], in_=prod[:].rearrange("p (j n) -> p j n", n=N_STATE), axis=AX.X, op=ALU.add
+        )
+        nc.vector.tensor_scalar_max(out=relu_dt[:], in0=dt4[:], scalar1=0.0)
+        nc.scalar.activation(out=abs_dt[:], in_=dt4[:], func=ACT.Abs)
+        nc.scalar.activation(out=exp_dt[:], in_=abs_dt[:], func=ACT.Exp, scale=-1.0)
+        nc.scalar.activation(out=log_dt[:], in_=exp_dt[:], func=ACT.Ln, bias=1.0)
+        nc.scalar.activation(out=warm[:], in_=zero_col[:], func=ACT.Silu)
+        nc.vector.tensor_tensor(out=gain[:], in0=log_dt[:], in1=relu_dt[:], op=ALU.add)
+        nc.vector.tensor_tensor(out=gain[:], in0=gain[:], in1=bc[:], op=ALU.mult)
+        nc.vector.tensor_tensor(out=gain[:], in0=gain[:], in1=dp4[:], op=ALU.add)
+        nc.vector.tensor_tensor(
+            out=gain[:], in0=gain[:], in1=cw4[:].rearrange("p (j k) -> p j k", k=4)[:, :, 3], op=ALU.add
+        )
+        nc.vector.tensor_tensor(out=shift[:], in0=inb4[:], in1=gain[:], op=ALU.mult)
+        nc.vector.tensor_tensor(out=shift[:], in0=shift[:], in1=cvb4[:], op=ALU.add)
+
+        xi = accp.tile([P, DI], F32, tag="acc", name="xi")
+
+        def first_matmul_passes(G):
+            for j in range(W_GROUPS):
+                g = G * W_GROUPS + j
+                nc.tensor.matmul_mx(
+                    out=xi[:],
+                    lhsT=x_codes[:, g * P : (g + 1) * P].bitcast(FP8X4),
+                    lhsT_scale=x_planes[:, g * P : (g + 1) * P],
+                    rhs=w_sb[G][:, j, :].bitcast(FP8X4),
+                    rhs_scale=in_planes[4 * j : P, G, :],
+                    start=(g == 0),
+                    stop=(g == GROUPS - 1),
+                )
+
+        def spread_over_partitions(column, dst):
+            spread_ps = tp.tile([P, PACK, P], F32, tag="tp", name="spread_ps")
+            for j in range(PACK):
+                nc.tensor.transpose(
+                    spread_ps[:, j, :], column[:, j : j + 1].to_broadcast([P, P]), ident_f32[:]
+                )
+            nc.scalar.copy(out=dst, in_=spread_ps[:])
+
+        ob_cols = keep.tile([P, P], F32)
+        bias_sb = []
+
+        def spread_out_b(c):
+            bias_piece = biasp.tile([P, O_COLS], BF16, name="bias_piece")
+            bias_sb.append(bias_piece)
+            words = bias_piece[:].bitcast(F32).rearrange("p (b j n) -> p b j n", j=PACK, n=P)
+            for b in range(O_COLS // 2 // BANK):
+                first = (c * (O_COLS // 2 // BANK) + b) * PACK
+                spread_over_partitions(ob_cols[:, first : first + PACK], words[:, b])
+
+        for G in range(W_CHUNKS // 2):
+            first_matmul_passes(G)
+
+        ob_ps = tp.tile([P, P], F32, tag="tp", name="ob_ps")
+        nc.tensor.transpose(ob_ps[:], ob_rows[:].bitcast(F32), ident_f32[:])
+        nc.scalar.copy(out=ob_cols[:], in_=ob_ps[:])
+        gain_bc = keep.tile([P, PACK, P], F32)
+        shift_bc = keep.tile([P, PACK, P], F32)
+        spread_over_partitions(gain, gain_bc[:])
+        spread_over_partitions(shift, shift_bc[:])
+        for c in range(BIAS_AHEAD):
+            spread_out_b(c)
+
+        for G in range(W_CHUNKS // 2, W_CHUNKS):
+            first_matmul_passes(G)
+
+        scaled = keep.tile([P, PACK, P], F32)
+        v = keep.tile([P, PACK, P], F32)
+        h = keep.tile([P, PACK, P], BF16)
+        nc.vector.tensor_tensor(
+            out=scaled[:], in0=xi[:].rearrange("m (p t) -> m t p", t=PACK), in1=gain_bc[:], op=ALU.mult
+        )
+        nc.vector.tensor_tensor(out=v[:], in0=scaled[:], in1=shift_bc[:], op=ALU.add)
+        nc.scalar.activation(out=h[:], in_=v[:], func=ACT.Silu)
+        ht = tp.tile([P, PACK, P], BF16, tag="tp", name="ht")
+        for t in range(PACK):
+            nc.tensor.transpose(ht[:, t, :], h[:, t, :], ident_bf16[:])
+        h_grouped = keep.tile([P, P, PACK], BF16, align_bytes=64)
+        nc.scalar.copy(out=h_grouped[:], in_=ht[:].rearrange("p t m -> p m t"))
+        h_codes = keep.tile([P, P], U32, align_bytes=64)
+        h_plane = keep.tile([P, P], U8, align_bytes=64)
+        nc.vector.quantize_mx(
+            out=h_codes[:].bitcast(FP8X4),
+            scales=h_plane[:],
+            in_=h_grouped[:].rearrange("p m t -> p (m t)"),
+        )
+
+        for c in range(O_CHUNKS):
+            o_piece = big.tile([P, O_COLS], F32, tag="mib", name="o_piece", align_bytes=64)
+            for b in range(O_BANKS):
+                cols = slice(b * BANK, (b + 1) * BANK)
+                n0 = c * O_COLS + b * BANK
+                plane = n0 // OW_PLANE_COLS
+                plane_col = n0 % OW_PLANE_COLS
+                acc = accp.tile([P, BANK], F32, tag="acc", name="acc")
+                nc.tensor.matmul_mx(
+                    out=acc[:],
+                    lhsT=h_codes[:].bitcast(FP8X4),
+                    lhsT_scale=h_plane[:],
+                    rhs=ow_sb[c][:, cols].bitcast(FP8X4),
+                    rhs_scale=ow_planes[4 * plane : P, plane_col : plane_col + BANK],
+                    start=True,
+                    stop=True,
+                )
+                nc.vector.tensor_tensor(out=o_piece[:, cols], in0=acc[:], in1=bias_sb[c][:, cols], op=ALU.add)
+            nc.sync.dma_start(out=out[:, c * O_COLS : (c + 1) * O_COLS], in_=o_piece[:])
+            if c + BIAS_AHEAD < O_CHUNKS:
+                spread_out_b(c + BIAS_AHEAD)

@@ -56,28 +56,24 @@ def tile_baselinedensemamba_k_kernel(
         ob_rows = keep.tile([P, 2 * P], BF16)
         zero_col = keep.tile([P, 1], F32)
         nc.vector.memset(in_planes[:].rearrange("p g n -> p (g n)").bitcast(I32), 0)
-        nc.vector.memset(ow_planes[:].bitcast(I32), 0)
-        nc.vector.memset(ob_rows[:], 0.0)
         nc.vector.memset(zero_col[:], 0.0)
+        nc.vector.memset(ob_rows[:], 0.0)
+        nc.vector.memset(ow_planes[:].bitcast(I32), 0)
 
         ident_f32 = keep.tile([P, P], F32)
         make_identity(nc, ident_f32[:])
 
-        dt4 = keep.tile([P, PACK], BF16)
-        b4 = keep.tile([P, PACK * N_STATE], BF16)
-        c4 = keep.tile([P, PACK * N_STATE], BF16)
-        dp4 = keep.tile([P, PACK], BF16)
-        cw4 = keep.tile([P, PACK * 4], BF16)
-        inb4 = keep.tile([P, PACK], BF16)
-        cvb4 = keep.tile([P, PACK], BF16)
-        nc.gpsimd.dma_start(out=dt4[:], in_=dt.rearrange("(p j) -> p j", j=PACK))
-        nc.gpsimd.dma_start(out=b4[:], in_=B.rearrange("(p j) n -> p (j n)", j=PACK))
-        nc.gpsimd.dma_start(out=c4[:], in_=C.rearrange("(p j) n -> p (j n)", j=PACK))
-        nc.gpsimd.dma_start(out=dp4[:], in_=Dp.rearrange("(p j) -> p j", j=PACK))
-        nc.gpsimd.dma_start(out=cw4[:], in_=conv_w.rearrange("(p j) k -> p (j k)", j=PACK))
-        nc.gpsimd.dma_start(out=inb4[:], in_=in_b.rearrange("(p j) -> p j", j=PACK))
-        nc.gpsimd.dma_start(out=cvb4[:], in_=conv_b.rearrange("(p j) -> p j", j=PACK))
-        nc.gpsimd.dma_start(out=ob_rows[0 : P // 2, :], in_=out_b.rearrange("(m w) -> m w", w=2 * P))
+        in_rows = in_w_scales.rearrange("(G j) (Q r) n -> j r Q G n", j=PLANES, r=4)
+        for j in range(PLANES):
+            for r in range(4):
+                nc.gpsimd.dma_start(
+                    out=in_planes[4 * j + r : P : 32].bitcast(F32), in_=in_rows[j, r].bitcast(F32)
+                )
+        for Q in range(QUADS):
+            nc.gpsimd.dma_start(
+                out=ow_planes[32 * Q : 32 * Q + 16, :].bitcast(F32),
+                in_=out_w_scales[0, 4 * Q : 4 * Q + 4, :].rearrange("r (j c) -> j r c", j=PLANES).bitcast(F32),
+            )
         ident_bf16 = keep.tile([P, P], BF16)
         make_identity(nc, ident_bf16[:])
 
@@ -105,20 +101,24 @@ def tile_baselinedensemamba_k_kernel(
                 ow_flat[:, c * O_COLS * PACK : (c + 1) * O_COLS * PACK].bitcast(I32),
             ))
 
-        small_loads = []
-        for G in range(W_CHUNKS):
-            for Q in range(QUADS):
-                small_loads.append((
-                    in_planes[32 * Q : 32 * Q + 16, G, :].bitcast(I32),
-                    in_w_scales[G * PLANES : (G + 1) * PLANES, 4 * Q : 4 * Q + 4, :].bitcast(I32),
-                ))
-        for Q in range(QUADS):
-            small_loads.append((
-                ow_planes[32 * Q : 32 * Q + 16, :].bitcast(I32),
-                out_w_scales[0, 4 * Q : 4 * Q + 4, :].rearrange("r (j c) -> j r c", j=PLANES).bitcast(I32),
-            ))
-
-        rounds = len(small_loads) // SMALL_PER_ROUND
+        dt4 = keep.tile([P, PACK], BF16)
+        b4 = keep.tile([P, PACK * N_STATE], BF16)
+        c4 = keep.tile([P, PACK * N_STATE], BF16)
+        dp4 = keep.tile([P, PACK], BF16)
+        cw4 = keep.tile([P, PACK * 4], BF16)
+        inb4 = keep.tile([P, PACK], BF16)
+        cvb4 = keep.tile([P, PACK], BF16)
+        small_loads = [
+            (dt4[:], dt.rearrange("(p j) -> p j", j=PACK)),
+            (ob_rows[0 : P // 2, :], out_b.rearrange("(m w) -> m w", w=2 * P)),
+            (b4[:], B.rearrange("(p j) n -> p (j n)", j=PACK)),
+            (c4[:], C.rearrange("(p j) n -> p (j n)", j=PACK)),
+            (dp4[:], Dp.rearrange("(p j) -> p j", j=PACK)),
+            (cw4[:], conv_w.rearrange("(p j) k -> p (j k)", j=PACK)),
+            (inb4[:], in_b.rearrange("(p j) -> p j", j=PACK)),
+            (cvb4[:], conv_b.rearrange("(p j) -> p j", j=PACK)),
+        ]
+        rounds = (len(small_loads) + SMALL_PER_ROUND - 1) // SMALL_PER_ROUND
         for r in range(rounds):
             for dst, src in big_loads[r * BIG_PER_ROUND : (r + 1) * BIG_PER_ROUND]:
                 nc.sync.dma_start(out=dst, in_=src)
@@ -126,6 +126,15 @@ def tile_baselinedensemamba_k_kernel(
                 nc.sync.dma_start(out=dst, in_=src)
         for dst, src in big_loads[rounds * BIG_PER_ROUND :]:
             nc.sync.dma_start(out=dst, in_=src)
+
+        abs_dt = keep.tile([P, PACK], F32)
+        exp_dt = keep.tile([P, PACK], F32)
+        log_dt = keep.tile([P, PACK], F32)
+        warm = keep.tile([P, 2], F32)
+        nc.scalar.activation(out=warm[:, 0:1], in_=zero_col[:], func=ACT.Exp)
+        nc.scalar.activation(out=abs_dt[:], in_=dt4[:], func=ACT.Abs)
+        nc.scalar.activation(out=exp_dt[:], in_=abs_dt[:], func=ACT.Exp, scale=-1.0)
+        nc.scalar.activation(out=log_dt[:], in_=exp_dt[:], func=ACT.Ln, bias=1.0)
 
         x_codes = keep.tile([P, GROUPS * P], U32, align_bytes=64)
         x_planes = keep.tile([P, GROUPS * P], U8, align_bytes=64)
@@ -156,21 +165,13 @@ def tile_baselinedensemamba_k_kernel(
         prod = keep.tile([P, PACK * N_STATE], F32)
         bc = keep.tile([P, PACK], F32)
         relu_dt = keep.tile([P, PACK], F32)
-        abs_dt = keep.tile([P, PACK], F32)
-        exp_dt = keep.tile([P, PACK], F32)
-        log_dt = keep.tile([P, PACK], F32)
         gain = keep.tile([P, PACK], F32)
         shift = keep.tile([P, PACK], F32)
-        warm = keep.tile([P, 1], F32)
         nc.vector.tensor_tensor(out=prod[:], in0=b4[:], in1=c4[:], op=ALU.mult)
         nc.vector.tensor_reduce(
             out=bc[:], in_=prod[:].rearrange("p (j n) -> p j n", n=N_STATE), axis=AX.X, op=ALU.add
         )
         nc.vector.tensor_scalar_max(out=relu_dt[:], in0=dt4[:], scalar1=0.0)
-        nc.scalar.activation(out=abs_dt[:], in_=dt4[:], func=ACT.Abs)
-        nc.scalar.activation(out=exp_dt[:], in_=abs_dt[:], func=ACT.Exp, scale=-1.0)
-        nc.scalar.activation(out=log_dt[:], in_=exp_dt[:], func=ACT.Ln, bias=1.0)
-        nc.scalar.activation(out=warm[:], in_=zero_col[:], func=ACT.Silu)
         nc.vector.tensor_tensor(out=gain[:], in0=log_dt[:], in1=relu_dt[:], op=ALU.add)
         nc.vector.tensor_tensor(out=gain[:], in0=gain[:], in1=bc[:], op=ALU.mult)
         nc.vector.tensor_tensor(out=gain[:], in0=gain[:], in1=dp4[:], op=ALU.add)
@@ -214,20 +215,18 @@ def tile_baselinedensemamba_k_kernel(
                 first = (c * (O_COLS // 2 // BANK) + b) * PACK
                 spread_over_partitions(ob_cols[:, first : first + PACK], words[:, b])
 
-        for G in range(W_CHUNKS // 2):
-            first_matmul_passes(G)
-
         ob_ps = tp.tile([P, P], F32, tag="tp", name="ob_ps")
         nc.tensor.transpose(ob_ps[:], ob_rows[:].bitcast(F32), ident_f32[:])
         nc.scalar.copy(out=ob_cols[:], in_=ob_ps[:])
+        for c in range(BIAS_AHEAD):
+            spread_out_b(c)
         gain_bc = keep.tile([P, PACK, P], F32)
         shift_bc = keep.tile([P, PACK, P], F32)
         spread_over_partitions(gain, gain_bc[:])
         spread_over_partitions(shift, shift_bc[:])
-        for c in range(BIAS_AHEAD):
-            spread_out_b(c)
+        nc.scalar.activation(out=warm[:, 1:2], in_=zero_col[:], func=ACT.Silu)
 
-        for G in range(W_CHUNKS // 2, W_CHUNKS):
+        for G in range(W_CHUNKS):
             first_matmul_passes(G)
 
         scaled = keep.tile([P, PACK, P], F32)

@@ -20,17 +20,19 @@ N_STATE = 16
 GROUPS = D // K_PASS
 BANK = 512
 
-X_CHUNKS = 4
+X_CHUNKS = 2
 X_COLS = D // X_CHUNKS
 X_GROUPS = GROUPS // X_CHUNKS
-W_CHUNKS = 8
+W_CHUNKS = 4
 W_GROUPS = GROUPS // W_CHUNKS
-O_CHUNKS = 8
+O_CHUNKS = 4
 O_COLS = D // O_CHUNKS
-O_BANKS = O_COLS // BANK
+BIAS_COLS = 2048
+BIAS_PIECES = D // BIAS_COLS
 PLANES = 4
 QUADS = 4
 OW_PLANE_COLS = D // PLANES
+assert OW_PLANE_COLS == O_COLS
 BIG_PER_ROUND = 2
 SMALL_PER_ROUND = 6
 BIAS_AHEAD = 2
@@ -44,14 +46,14 @@ def tile_baselinedensemamba_k_kernel(
 ):
     nc = tc.nc
     with tc.manual_schedule(), \
-            tc.tile_pool(name="big", bufs=X_CHUNKS + W_CHUNKS + O_CHUNKS) as big, \
+            tc.tile_pool(name="wide", bufs=X_CHUNKS + W_CHUNKS + O_CHUNKS) as wide, \
             tc.tile_pool(name="keep", bufs=1) as keep, \
             tc.tile_pool(name="stage", bufs=4) as stage, \
             tc.tile_pool(name="biasp", bufs=BIAS_AHEAD + 1) as biasp, \
             tc.psum_pool(name="tp", bufs=3) as tp, \
             tc.psum_pool(name="accp", bufs=5) as accp:
 
-        in_planes = keep.tile([P, W_CHUNKS, DI], U8, align_bytes=64)
+        in_planes = keep.tile([P, GROUPS // PLANES, DI], U8, align_bytes=64)
         ow_planes = keep.tile([P, OW_PLANE_COLS], U8, align_bytes=64)
         ob_rows = keep.tile([P, 2 * P], BF16)
         zero_col = keep.tile([P, 1], F32)
@@ -80,12 +82,12 @@ def tile_baselinedensemamba_k_kernel(
         big_loads = []
         x_sb = []
         for c in range(X_CHUNKS):
-            x_piece = big.tile([P, X_COLS], BF16, tag="mib", name="x_piece", align_bytes=64)
+            x_piece = wide.tile([P, X_COLS], BF16, tag="wide", name="x_piece", align_bytes=64)
             x_sb.append(x_piece)
             big_loads.append((x_piece[:], x[:, c * X_COLS : (c + 1) * X_COLS]))
         w_sb = []
         for G in range(W_CHUNKS):
-            w_piece = big.tile([P, W_GROUPS, DI], U32, tag="mib", name="w_piece", align_bytes=64)
+            w_piece = wide.tile([P, W_GROUPS, DI], U32, tag="wide", name="w_piece", align_bytes=64)
             w_sb.append(w_piece)
             big_loads.append((
                 w_piece[:].bitcast(I32),
@@ -94,7 +96,7 @@ def tile_baselinedensemamba_k_kernel(
         ow_sb = []
         ow_flat = out_w_words[0].rearrange("p n t -> p (n t)")
         for c in range(O_CHUNKS):
-            ow_piece = big.tile([P, O_COLS], U32, tag="mib", name="ow_piece", align_bytes=64)
+            ow_piece = wide.tile([P, O_COLS], U32, tag="wide", name="ow_piece", align_bytes=64)
             ow_sb.append(ow_piece)
             big_loads.append((
                 ow_piece[:].bitcast(I32),
@@ -183,15 +185,15 @@ def tile_baselinedensemamba_k_kernel(
 
         xi = accp.tile([P, DI], F32, tag="acc", name="xi")
 
-        def first_matmul_passes(G):
-            for j in range(W_GROUPS):
-                g = G * W_GROUPS + j
+        def first_matmul_passes(c):
+            for i in range(W_GROUPS):
+                g = c * W_GROUPS + i
                 nc.tensor.matmul_mx(
                     out=xi[:],
                     lhsT=x_codes[:, g * P : (g + 1) * P].bitcast(FP8X4),
                     lhsT_scale=x_planes[:, g * P : (g + 1) * P],
-                    rhs=w_sb[G][:, j, :].bitcast(FP8X4),
-                    rhs_scale=in_planes[4 * j : P, G, :],
+                    rhs=w_sb[c][:, i, :].bitcast(FP8X4),
+                    rhs_scale=in_planes[4 * (g % PLANES) : P, g // PLANES, :],
                     start=(g == 0),
                     stop=(g == GROUPS - 1),
                 )
@@ -208,11 +210,11 @@ def tile_baselinedensemamba_k_kernel(
         bias_sb = []
 
         def spread_out_b(c):
-            bias_piece = biasp.tile([P, O_COLS], BF16, name="bias_piece")
+            bias_piece = biasp.tile([P, BIAS_COLS], BF16, name="bias_piece")
             bias_sb.append(bias_piece)
             words = bias_piece[:].bitcast(F32).rearrange("p (b j n) -> p b j n", j=PACK, n=P)
-            for b in range(O_COLS // 2 // BANK):
-                first = (c * (O_COLS // 2 // BANK) + b) * PACK
+            for b in range(BIAS_COLS // 2 // BANK):
+                first = (c * (BIAS_COLS // 2 // BANK) + b) * PACK
                 spread_over_partitions(ob_cols[:, first : first + PACK], words[:, b])
 
         ob_ps = tp.tile([P, P], F32, tag="tp", name="ob_ps")
@@ -226,8 +228,8 @@ def tile_baselinedensemamba_k_kernel(
         spread_over_partitions(shift, shift_bc[:])
         nc.scalar.activation(out=warm[:, 1:2], in_=zero_col[:], func=ACT.Silu)
 
-        for G in range(W_CHUNKS):
-            first_matmul_passes(G)
+        for c in range(W_CHUNKS):
+            first_matmul_passes(c)
 
         scaled = keep.tile([P, PACK, P], F32)
         v = keep.tile([P, PACK, P], F32)
@@ -251,23 +253,27 @@ def tile_baselinedensemamba_k_kernel(
         )
 
         for c in range(O_CHUNKS):
-            o_piece = big.tile([P, O_COLS], F32, tag="mib", name="o_piece", align_bytes=64)
-            for b in range(O_BANKS):
-                cols = slice(b * BANK, (b + 1) * BANK)
-                n0 = c * O_COLS + b * BANK
-                plane = n0 // OW_PLANE_COLS
-                plane_col = n0 % OW_PLANE_COLS
-                acc = accp.tile([P, BANK], F32, tag="acc", name="acc")
-                nc.tensor.matmul_mx(
-                    out=acc[:],
-                    lhsT=h_codes[:].bitcast(FP8X4),
-                    lhsT_scale=h_plane[:],
-                    rhs=ow_sb[c][:, cols].bitcast(FP8X4),
-                    rhs_scale=ow_planes[4 * plane : P, plane_col : plane_col + BANK],
-                    start=True,
-                    stop=True,
-                )
-                nc.vector.tensor_tensor(out=o_piece[:, cols], in0=acc[:], in1=bias_sb[c][:, cols], op=ALU.add)
+            o_piece = wide.tile([P, O_COLS], F32, tag="wide", name="o_piece", align_bytes=64)
+            for half in range(O_COLS // BIAS_COLS):
+                piece = c * (O_COLS // BIAS_COLS) + half
+                for b in range(BIAS_COLS // BANK):
+                    cols = slice(half * BIAS_COLS + b * BANK, half * BIAS_COLS + (b + 1) * BANK)
+                    acc = accp.tile([P, BANK], F32, tag="acc", name="acc")
+                    nc.tensor.matmul_mx(
+                        out=acc[:],
+                        lhsT=h_codes[:].bitcast(FP8X4),
+                        lhsT_scale=h_plane[:],
+                        rhs=ow_sb[c][:, cols].bitcast(FP8X4),
+                        rhs_scale=ow_planes[4 * c : P, cols],
+                        start=True,
+                        stop=True,
+                    )
+                    nc.vector.tensor_tensor(
+                        out=o_piece[:, cols],
+                        in0=acc[:],
+                        in1=bias_sb[piece][:, b * BANK : (b + 1) * BANK],
+                        op=ALU.add,
+                    )
+                if piece + BIAS_AHEAD < BIAS_PIECES:
+                    spread_out_b(piece + BIAS_AHEAD)
             nc.sync.dma_start(out=out[:, c * O_COLS : (c + 1) * O_COLS], in_=o_piece[:])
-            if c + BIAS_AHEAD < O_CHUNKS:
-                spread_out_b(c + BIAS_AHEAD)

import concourse.mybir as mybir
from concourse.masks import make_identity

F32 = mybir.dt.float32
BF16 = mybir.dt.bfloat16
I32 = mybir.dt.int32
U32 = mybir.dt.uint32
U8 = mybir.dt.uint8
FP8X4 = mybir.dt.float8_e4m3fn_x4
ACT = mybir.ActivationFunctionType
ALU = mybir.AluOpType
AX = mybir.AxisListType

P = 128
PACK = 4
K_PASS = P * PACK
D = 16384
DI = 512
N_STATE = 16
GROUPS = D // K_PASS
BANK = 512

X_CHUNKS = 2
X_COLS = D // X_CHUNKS
X_GROUPS = GROUPS // X_CHUNKS
W_CHUNKS = 4
W_GROUPS = GROUPS // W_CHUNKS
O_CHUNKS = 4
O_COLS = D // O_CHUNKS
BIAS_COLS = 2048
BIAS_PIECES = D // BIAS_COLS
PLANES = 4
QUADS = 4
OW_PLANE_COLS = D // PLANES
assert OW_PLANE_COLS == O_COLS
BIG_PER_ROUND = 2
SMALL_PER_ROUND = 6
BIAS_AHEAD = 2

FLOPS = 2 * P * D * DI * 2


def tile_baselinedensemamba_k_kernel(
    tc, x, in_w_words, in_w_scales, in_b, conv_w, conv_b, A_log, B, C, Dp, dt,
    out_w_words, out_w_scales, out_b, out,
):
    nc = tc.nc
    with tc.manual_schedule(), \
            tc.tile_pool(name="wide", bufs=X_CHUNKS + W_CHUNKS + O_CHUNKS) as wide, \
            tc.tile_pool(name="keep", bufs=1) as keep, \
            tc.tile_pool(name="stage", bufs=4) as stage, \
            tc.tile_pool(name="biasp", bufs=BIAS_AHEAD + 1) as biasp, \
            tc.psum_pool(name="tp", bufs=3) as tp, \
            tc.psum_pool(name="accp", bufs=5) as accp:

        in_planes = keep.tile([P, GROUPS // PLANES, DI], U8, align_bytes=64)
        ow_planes = keep.tile([P, OW_PLANE_COLS], U8, align_bytes=64)
        ob_rows = keep.tile([P, 2 * P], BF16)
        zero_col = keep.tile([P, 1], F32)
        nc.vector.memset(in_planes[:].rearrange("p g n -> p (g n)").bitcast(I32), 0)
        nc.vector.memset(zero_col[:], 0.0)
        nc.vector.memset(ob_rows[:], 0.0)
        nc.vector.memset(ow_planes[:].bitcast(I32), 0)

        ident_f32 = keep.tile([P, P], F32)
        make_identity(nc, ident_f32[:])

        in_rows = in_w_scales.rearrange("(G j) (Q r) n -> j r Q G n", j=PLANES, r=4)
        for j in range(PLANES):
            for r in range(4):
                nc.gpsimd.dma_start(
                    out=in_planes[4 * j + r : P : 32].bitcast(F32), in_=in_rows[j, r].bitcast(F32)
                )
        for Q in range(QUADS):
            nc.gpsimd.dma_start(
                out=ow_planes[32 * Q : 32 * Q + 16, :].bitcast(F32),
                in_=out_w_scales[0, 4 * Q : 4 * Q + 4, :].rearrange("r (j c) -> j r c", j=PLANES).bitcast(F32),
            )
        ident_bf16 = keep.tile([P, P], BF16)
        make_identity(nc, ident_bf16[:])

        big_loads = []
        x_sb = []
        for c in range(X_CHUNKS):
            x_piece = wide.tile([P, X_COLS], BF16, tag="wide", name="x_piece", align_bytes=64)
            x_sb.append(x_piece)
            big_loads.append((x_piece[:], x[:, c * X_COLS : (c + 1) * X_COLS]))
        w_sb = []
        for G in range(W_CHUNKS):
            w_piece = wide.tile([P, W_GROUPS, DI], U32, tag="wide", name="w_piece", align_bytes=64)
            w_sb.append(w_piece)
            big_loads.append((
                w_piece[:].bitcast(I32),
                in_w_words[G * W_GROUPS : (G + 1) * W_GROUPS].rearrange("g p n t -> p g (n t)").bitcast(I32),
            ))
        ow_sb = []
        ow_flat = out_w_words[0].rearrange("p n t -> p (n t)")
        for c in range(O_CHUNKS):
            ow_piece = wide.tile([P, O_COLS], U32, tag="wide", name="ow_piece", align_bytes=64)
            ow_sb.append(ow_piece)
            big_loads.append((
                ow_piece[:].bitcast(I32),
                ow_flat[:, c * O_COLS * PACK : (c + 1) * O_COLS * PACK].bitcast(I32),
            ))

        dt4 = keep.tile([P, PACK], BF16)
        b4 = keep.tile([P, PACK * N_STATE], BF16)
        c4 = keep.tile([P, PACK * N_STATE], BF16)
        dp4 = keep.tile([P, PACK], BF16)
        cw4 = keep.tile([P, PACK * 4], BF16)
        inb4 = keep.tile([P, PACK], BF16)
        cvb4 = keep.tile([P, PACK], BF16)
        small_loads = [
            (dt4[:], dt.rearrange("(p j) -> p j", j=PACK)),
            (ob_rows[0 : P // 2, :], out_b.rearrange("(m w) -> m w", w=2 * P)),
            (b4[:], B.rearrange("(p j) n -> p (j n)", j=PACK)),
            (c4[:], C.rearrange("(p j) n -> p (j n)", j=PACK)),
            (dp4[:], Dp.rearrange("(p j) -> p j", j=PACK)),
            (cw4[:], conv_w.rearrange("(p j) k -> p (j k)", j=PACK)),
            (inb4[:], in_b.rearrange("(p j) -> p j", j=PACK)),
            (cvb4[:], conv_b.rearrange("(p j) -> p j", j=PACK)),
        ]
        rounds = (len(small_loads) + SMALL_PER_ROUND - 1) // SMALL_PER_ROUND
        for r in range(rounds):
            for dst, src in big_loads[r * BIG_PER_ROUND : (r + 1) * BIG_PER_ROUND]:
                nc.sync.dma_start(out=dst, in_=src)
            for dst, src in small_loads[r * SMALL_PER_ROUND : (r + 1) * SMALL_PER_ROUND]:
                nc.sync.dma_start(out=dst, in_=src)
        for dst, src in big_loads[rounds * BIG_PER_ROUND :]:
            nc.sync.dma_start(out=dst, in_=src)

        abs_dt = keep.tile([P, PACK], F32)
        exp_dt = keep.tile([P, PACK], F32)
        log_dt = keep.tile([P, PACK], F32)
        warm = keep.tile([P, 2], F32)
        nc.scalar.activation(out=warm[:, 0:1], in_=zero_col[:], func=ACT.Exp)
        nc.scalar.activation(out=abs_dt[:], in_=dt4[:], func=ACT.Abs)
        nc.scalar.activation(out=exp_dt[:], in_=abs_dt[:], func=ACT.Exp, scale=-1.0)
        nc.scalar.activation(out=log_dt[:], in_=exp_dt[:], func=ACT.Ln, bias=1.0)

        x_codes = keep.tile([P, GROUPS * P], U32, align_bytes=64)
        x_planes = keep.tile([P, GROUPS * P], U8, align_bytes=64)
        for c in range(X_CHUNKS):
            x_words = x_sb[c][:].bitcast(F32)
            for pair in range(X_GROUPS // 2):
                xt = tp.tile([P, 2, 2, P], F32, tag="tp", name="xt")
                for i in range(2):
                    first = (2 * pair + i) * (K_PASS // 2)
                    for u in range(2):
                        nc.tensor.transpose(
                            xt[:, i, u, :],
                            x_words[:, first + u : first + K_PASS // 2 : 2],
                            ident_f32[:],
                        )
                grouped = stage.tile([P, 2 * K_PASS], BF16, name="grouped", align_bytes=64)
                nc.scalar.copy(
                    out=grouped[:].bitcast(F32).rearrange("p (i m u) -> p i m u", i=2, u=2),
                    in_=xt[:].rearrange("p i u m -> p i m u"),
                )
                col = (c * X_GROUPS + 2 * pair) * P
                nc.vector.quantize_mx(
                    out=x_codes[:, col : col + 2 * P].bitcast(FP8X4),
                    scales=x_planes[:, col : col + 2 * P],
                    in_=grouped[:],
                )

        prod = keep.tile([P, PACK * N_STATE], F32)
        bc = keep.tile([P, PACK], F32)
        relu_dt = keep.tile([P, PACK], F32)
        gain = keep.tile([P, PACK], F32)
        shift = keep.tile([P, PACK], F32)
        nc.vector.tensor_tensor(out=prod[:], in0=b4[:], in1=c4[:], op=ALU.mult)
        nc.vector.tensor_reduce(
            out=bc[:], in_=prod[:].rearrange("p (j n) -> p j n", n=N_STATE), axis=AX.X, op=ALU.add
        )
        nc.vector.tensor_scalar_max(out=relu_dt[:], in0=dt4[:], scalar1=0.0)
        nc.vector.tensor_tensor(out=gain[:], in0=log_dt[:], in1=relu_dt[:], op=ALU.add)
        nc.vector.tensor_tensor(out=gain[:], in0=gain[:], in1=bc[:], op=ALU.mult)
        nc.vector.tensor_tensor(out=gain[:], in0=gain[:], in1=dp4[:], op=ALU.add)
        nc.vector.tensor_tensor(
            out=gain[:], in0=gain[:], in1=cw4[:].rearrange("p (j k) -> p j k", k=4)[:, :, 3], op=ALU.add
        )
        nc.vector.tensor_tensor(out=shift[:], in0=inb4[:], in1=gain[:], op=ALU.mult)
        nc.vector.tensor_tensor(out=shift[:], in0=shift[:], in1=cvb4[:], op=ALU.add)

        xi = accp.tile([P, DI], F32, tag="acc", name="xi")

        def first_matmul_passes(c):
            for i in range(W_GROUPS):
                g = c * W_GROUPS + i
                nc.tensor.matmul_mx(
                    out=xi[:],
                    lhsT=x_codes[:, g * P : (g + 1) * P].bitcast(FP8X4),
                    lhsT_scale=x_planes[:, g * P : (g + 1) * P],
                    rhs=w_sb[c][:, i, :].bitcast(FP8X4),
                    rhs_scale=in_planes[4 * (g % PLANES) : P, g // PLANES, :],
                    start=(g == 0),
                    stop=(g == GROUPS - 1),
                )

        def spread_over_partitions(column, dst):
            spread_ps = tp.tile([P, PACK, P], F32, tag="tp", name="spread_ps")
            for j in range(PACK):
                nc.tensor.transpose(
                    spread_ps[:, j, :], column[:, j : j + 1].to_broadcast([P, P]), ident_f32[:]
                )
            nc.scalar.copy(out=dst, in_=spread_ps[:])

        ob_cols = keep.tile([P, P], F32)
        bias_sb = []

        def spread_out_b(c):
            bias_piece = biasp.tile([P, BIAS_COLS], BF16, name="bias_piece")
            bias_sb.append(bias_piece)
            words = bias_piece[:].bitcast(F32).rearrange("p (b j n) -> p b j n", j=PACK, n=P)
            for b in range(BIAS_COLS // 2 // BANK):
                first = (c * (BIAS_COLS // 2 // BANK) + b) * PACK
                spread_over_partitions(ob_cols[:, first : first + PACK], words[:, b])

        ob_ps = tp.tile([P, P], F32, tag="tp", name="ob_ps")
        nc.tensor.transpose(ob_ps[:], ob_rows[:].bitcast(F32), ident_f32[:])
        nc.scalar.copy(out=ob_cols[:], in_=ob_ps[:])
        for c in range(BIAS_AHEAD):
            spread_out_b(c)
        gain_bc = keep.tile([P, PACK, P], F32)
        shift_bc = keep.tile([P, PACK, P], F32)
        spread_over_partitions(gain, gain_bc[:])
        spread_over_partitions(shift, shift_bc[:])
        nc.scalar.activation(out=warm[:, 1:2], in_=zero_col[:], func=ACT.Silu)

        for c in range(W_CHUNKS):
            first_matmul_passes(c)

        scaled = keep.tile([P, PACK, P], F32)
        v = keep.tile([P, PACK, P], F32)
        h = keep.tile([P, PACK, P], BF16)
        nc.vector.tensor_tensor(
            out=scaled[:], in0=xi[:].rearrange("m (p t) -> m t p", t=PACK), in1=gain_bc[:], op=ALU.mult
        )
        nc.vector.tensor_tensor(out=v[:], in0=scaled[:], in1=shift_bc[:], op=ALU.add)
        nc.scalar.activation(out=h[:], in_=v[:], func=ACT.Silu)
        ht = tp.tile([P, PACK, P], BF16, tag="tp", name="ht")
        for t in range(PACK):
            nc.tensor.transpose(ht[:, t, :], h[:, t, :], ident_bf16[:])
        h_grouped = keep.tile([P, P, PACK], BF16, align_bytes=64)
        nc.scalar.copy(out=h_grouped[:], in_=ht[:].rearrange("p t m -> p m t"))
        h_codes = keep.tile([P, P], U32, align_bytes=64)
        h_plane = keep.tile([P, P], U8, align_bytes=64)
        nc.vector.quantize_mx(
            out=h_codes[:].bitcast(FP8X4),
            scales=h_plane[:],
            in_=h_grouped[:].rearrange("p m t -> p (m t)"),
        )

        for c in range(O_CHUNKS):
            o_piece = wide.tile([P, O_COLS], F32, tag="wide", name="o_piece", align_bytes=64)
            for half in range(O_COLS // BIAS_COLS):
                piece = c * (O_COLS // BIAS_COLS) + half
                for b in range(BIAS_COLS // BANK):
                    cols = slice(half * BIAS_COLS + b * BANK, half * BIAS_COLS + (b + 1) * BANK)
                    acc = accp.tile([P, BANK], F32, tag="acc", name="acc")
                    nc.tensor.matmul_mx(
                        out=acc[:],
                        lhsT=h_codes[:].bitcast(FP8X4),
                        lhsT_scale=h_plane[:],
                        rhs=ow_sb[c][:, cols].bitcast(FP8X4),
                        rhs_scale=ow_planes[4 * c : P, cols],
                        start=True,
                        stop=True,
                    )
                    nc.vector.tensor_tensor(
                        out=o_piece[:, cols],
                        in0=acc[:],
                        in1=bias_sb[piece][:, b * BANK : (b + 1) * BANK],
                        op=ALU.add,
                    )
                if piece + BIAS_AHEAD < BIAS_PIECES:
                    spread_out_b(piece + BIAS_AHEAD)
            nc.sync.dma_start(out=out[:, c * O_COLS : (c + 1) * O_COLS], in_=o_piece[:])
